import numpy as np
import ml_dtypes


def mxq(x, axis, fmt="e4m3"):
    dtype, down = {"e4m3": (ml_dtypes.float8_e4m3fn, 7), "e5m2": (ml_dtypes.float8_e5m2, 14)}[fmt]
    v = np.moveaxis(np.asarray(x, np.float32).astype(ml_dtypes.bfloat16).astype(np.float64), axis, -1)
    blocks = v.reshape(v.shape[:-1] + (-1, 32))
    amax = np.abs(blocks).max(-1, keepdims=True)
    byte = np.maximum(np.where(amax > 0, np.frexp(amax)[1] - 1 + 127, 0) - down, 1)
    scale = np.exp2(byte - 127.0)
    codes = (blocks / scale).astype(np.float32).astype(dtype).astype(np.float64)
    return np.moveaxis((codes * scale).reshape(v.shape), -1, axis)


WIDE = False


def mx_kscale(k):
    if not WIDE:
        return np.ones(k)
    levels = np.array([20, -20, 10, -10, 0])
    a = np.random.permutation(np.resize(levels, k // 512 * 4)).reshape(k // 512, 4)
    idx = np.arange(k)
    return np.exp2(a[idx // 512, idx % 128 // 32])


BF16 = ml_dtypes.bfloat16


def bf(x):
    return np.asarray(x, np.float32).astype(BF16)


def f64(x):
    return np.asarray(x).astype(np.float64)


B, IN_C, OUT_C, HM, HN, NL = 512, 512, 512, 512, 8, 3


def leaky(v, leak):
    return np.where(v < 0, v * leak, v)


def setup_inputs():
    s = mx_kscale(B)
    x0 = bf(np.random.standard_normal((B, IN_C)))
    W_im = bf(np.random.standard_normal((HN, IN_C, HM)) * 0.7 / np.sqrt(IN_C))
    W_in = bf(np.random.standard_normal((HM, IN_C, HN)) * 0.7 / np.sqrt(IN_C))
    leak_m = bf(np.random.uniform(-2.0, 2.0, HM))
    leak_n = bf(np.random.uniform(-2.0, 2.0, HN))
    g = bf(np.random.standard_normal((B, HN, HM)) * np.exp2(np.random.randint(-12, 1, (B, 1, 1))) / s[:, None, None])
    z_m = (f64(x0) @ f64(W_im).transpose(1, 0, 2).reshape(IN_C, HN * HM)).reshape(B, HN, HM)
    return {"x": bf(f64(x0) * s[:, None]), "W_im": W_im, "W_in": W_in, "leak_m": leak_m, "leak_n": leak_n,
            "z_m": np.asarray(z_m, np.float32), "grad_out": g}


def reference(x, W_im, W_in, leak_m, leak_n, z_m, grad_out):
    zm = f64(z_m)
    dz = f64(grad_out) * np.where(zm < 0, f64(leak_m), 1.0)
    dzq = mxq(dz.reshape(B, HN * HM), 0, "e5m2")
    xq = mxq(f64(x), 0, "e4m3")
    d = xq.T @ dzq
    return d.reshape(IN_C, HN, HM).transpose(1, 0, 2)

@@ -1,0 +1,142 @@
+from contextlib import ExitStack
+
+import concourse.mybir as mybir
+
+F32 = mybir.dt.float32
+BF16 = mybir.dt.bfloat16
+U32 = mybir.dt.uint32
+U8 = mybir.dt.uint8
+E4M3_X4 = mybir.dt.float8_e4m3fn_x4
+E5M2_X4 = mybir.dt.float8_e5m2_x4
+ALU = mybir.AluOpType
+
+P = 128
+PACK = 4
+B = P * PACK
+IN_C = 512
+HN = 8
+HM = 512
+I_TILES = IN_C // P
+
+FLOPS = 2 * B * IN_C * HN * HM
+BYTES = 2 * B * IN_C + 2 * HM + 4 * B * HN * HM + 2 * B * HN * HM + 4 * HN * IN_C * HM
+
+
+def tile_tensormoe_pa_v_kernel(tc, x, W_im, W_in, leak_m, leak_n, z_m, grad_out, out):
+    nc = tc.nc
+    x_rows = x.rearrange("(p j) i -> p j i", j=PACK)
+    z_rows = z_m.rearrange("(p j) n m -> p j n m", j=PACK)
+    g_rows = grad_out.rearrange("(p j) n m -> p j n m", j=PACK)
+
+    with ExitStack() as pools:
+        const = pools.enter_context(tc.tile_pool(name="const", bufs=1))
+        z_pool = pools.enter_context(tc.tile_pool(name="z", bufs=HN))
+        g_pool = pools.enter_context(tc.tile_pool(name="g", bufs=HN))
+        work = pools.enter_context(tc.tile_pool(name="work", bufs=3))
+        result_pool = pools.enter_context(tc.tile_pool(name="result", bufs=6))
+        psum_const = pools.enter_context(tc.psum_pool(name="psum_const", bufs=1))
+        psum = pools.enter_context(tc.psum_pool(name="psum", bufs=7))
+
+        z_tiles = []
+        g_tiles = []
+        slope_tiles = {}
+        dz_tiles = {}
+
+        def load_z(n):
+            z_n = z_pool.tile([P, PACK, HM], F32)
+            nc.sync.dma_start(out=z_n[:], in_=z_rows[:, :, n, :])
+            z_tiles.append(z_n)
+
+        def load_g(n):
+            g_n = g_pool.tile([P, PACK, HM], BF16)
+            nc.sync.dma_start(out=g_n[:], in_=g_rows[:, :, n, :])
+            g_tiles.append(g_n)
+
+        ones = const.tile([P, P], BF16)
+        nc.vector.memset(ones[:], 1.0)
+        leak_rows = const.tile([P, HM], BF16)
+        nc.vector.memset(leak_rows[:], 0.0)
+        nc.sync.dma_start(out=leak_rows[0:1, :], in_=leak_m.unsqueeze(0))
+        load_z(0)
+        load_z(1)
+        load_g(0)
+        x_raw = const.tile([P, PACK, IN_C], BF16)
+        nc.sync.dma_start(out=x_raw[:], in_=x_rows)
+        for n in range(1, HN):
+            if n + 1 < HN:
+                load_z(n + 1)
+            load_g(n)
+
+        leak_bank = psum_const.tile([P, HM], F32)
+        nc.tensor.matmul(out=leak_bank[:], lhsT=ones[:], rhs=leak_rows[:], start=True, stop=True)
+        leak_minus_1 = const.tile([P, HM], F32)
+        nc.vector.tensor_scalar_add(out=leak_minus_1[:], in0=leak_bank[:], scalar1=-1.0)
+
+        x_grouped = const.tile([P, I_TILES, P, PACK], BF16, align_bytes=64)
+        nc.scalar.copy(out=x_grouped[:], in_=x_raw[:].rearrange("p j (q a) -> p a q j", a=I_TILES))
+        x_codes = const.tile([P, IN_C], U32, align_bytes=64)
+        x_scales = const.tile([P, IN_C], U8, align_bytes=64)
+
+        def quantise_x():
+            nc.vector.quantize_mx(
+                out=x_codes[:].bitcast(E4M3_X4),
+                scales=x_scales[:],
+                in_=x_grouped[:].rearrange("p a q j -> p (a q j)"),
+            )
+
+        def slope_minus_1(n):
+            s_n = work.tile([P, HM, PACK], F32)
+            nc.vector.scalar_tensor_tensor(
+                out=s_n[:],
+                in0=z_tiles[n][:].rearrange("p j m -> p m j"),
+                scalar=0.0,
+                in1=leak_minus_1[:].unsqueeze(2).to_broadcast([P, HM, PACK]),
+                op0=ALU.is_lt,
+                op1=ALU.mult,
+            )
+            slope_tiles[n] = s_n
+
+        def gradient_times_slope(n):
+            dz_n = work.tile([P, HM, PACK], BF16, align_bytes=64)
+            nc.vector.scalar_tensor_tensor(
+                out=dz_n[:],
+                in0=slope_tiles[n][:],
+                scalar=1.0,
+                in1=g_tiles[n][:].rearrange("p j m -> p m j"),
+                op0=ALU.add,
+                op1=ALU.mult,
+            )
+            dz_tiles[n] = dz_n
+
+        def quantise_multiply_store(n):
+            dz_codes = work.tile([P, HM], U32, align_bytes=64)
+            dz_scales = work.tile([P, HM], U8, align_bytes=64)
+            nc.vector.quantize_mx(
+                out=dz_codes[:].bitcast(E5M2_X4),
+                scales=dz_scales[:],
+                in_=dz_tiles[n][:].rearrange("p m j -> p (m j)"),
+            )
+            result = result_pool.tile([P, I_TILES, HM], F32)
+            for a in range(I_TILES):
+                x_cols = slice(a * P, (a + 1) * P)
+                bank = psum.tile([P, HM], F32)
+                nc.tensor.matmul_mx(
+                    out=bank[:],
+                    lhsT=x_codes[:, x_cols].bitcast(E4M3_X4),
+                    lhsT_scale=x_scales[:, x_cols],
+                    rhs=dz_codes[:].bitcast(E5M2_X4),
+                    rhs_scale=dz_scales[:],
+                    start=True,
+                    stop=True,
+                )
+                nc.scalar.copy(out=result[:, a, :], in_=bank[:])
+            nc.sync.dma_start(out=out[n].rearrange("(q a) m -> q a m", a=I_TILES), in_=result[:])
+
+        slope_minus_1(0)
+        slope_minus_1(1)
+        quantise_x()
+        for n in range(HN):
+            gradient_times_slope(n)
+            if n + 2 < HN:
+                slope_minus_1(n + 2)
+            quantise_multiply_store(n)

@@ -17,6 +17,7 @@ IN_C = 512
 HN = 8
 HM = 512
 I_TILES = IN_C // P
+RUN = 4
 
 FLOPS = 2 * B * IN_C * HN * HM
 BYTES = 2 * B * IN_C + 2 * HM + 4 * B * HN * HM + 2 * B * HN * HM + 4 * HN * IN_C * HM
@@ -85,26 +86,31 @@ def tile_tensormoe_pa_v_kernel(tc, x, W_im, W_in, leak_m, leak_n, z_m, grad_out,
             )
 
         def slope_minus_1(n):
-            s_n = work.tile([P, HM, PACK], F32)
+            s_n = work.tile([P, PACK, HM], F32)
             nc.vector.scalar_tensor_tensor(
                 out=s_n[:],
-                in0=z_tiles[n][:].rearrange("p j m -> p m j"),
+                in0=z_tiles[n][:],
                 scalar=0.0,
-                in1=leak_minus_1[:].unsqueeze(2).to_broadcast([P, HM, PACK]),
+                in1=leak_minus_1[:].unsqueeze(1).to_broadcast([P, PACK, HM]),
                 op0=ALU.is_lt,
                 op1=ALU.mult,
             )
             slope_tiles[n] = s_n
 
         def gradient_times_slope(n):
-            dz_n = work.tile([P, HM, PACK], BF16, align_bytes=64)
+            dz_rows = work.tile([P, PACK, HM], BF16)
             nc.vector.scalar_tensor_tensor(
-                out=dz_n[:],
+                out=dz_rows[:],
                 in0=slope_tiles[n][:],
                 scalar=1.0,
-                in1=g_tiles[n][:].rearrange("p j m -> p m j"),
+                in1=g_tiles[n][:],
                 op0=ALU.add,
                 op1=ALU.mult,
+            )
+            dz_n = work.tile([P, HM, PACK], BF16, align_bytes=64)
+            nc.scalar.copy(
+                out=dz_n[:].rearrange("p (c r) j -> p c j r", r=RUN),
+                in_=dz_rows[:].rearrange("p j (c r) -> p c j r", r=RUN),
             )
             dz_tiles[n] = dz_n
 
@@ -134,9 +140,11 @@ def tile_tensormoe_pa_v_kernel(tc, x, W_im, W_in, leak_m, leak_n, z_m, grad_out,
 
         slope_minus_1(0)
         slope_minus_1(1)
+        gradient_times_slope(0)
         quantise_x()
         for n in range(HN):
-            gradient_times_slope(n)
             if n + 2 < HN:
                 slope_minus_1(n + 2)
+            if n + 1 < HN:
+                gradient_times_slope(n + 1)
             quantise_multiply_store(n)

@@ -15,6 +15,7 @@ PACK = 4
 B = P * PACK
 IN_C = 512
 HN = 8
+LAST = HN - 1
 HM = 512
 I_TILES = IN_C // P
 RUN = 4
@@ -29,54 +30,60 @@ def tile_tensormoe_pa_v_kernel(tc, x, W_im, W_in, leak_m, leak_n, z_m, grad_out,
     z_rows = z_m.rearrange("(p j) n m -> p j n m", j=PACK)
     g_rows = grad_out.rearrange("(p j) n m -> p j n m", j=PACK)
 
-    with ExitStack() as pools:
-        const = pools.enter_context(tc.tile_pool(name="const", bufs=1))
-        z_pool = pools.enter_context(tc.tile_pool(name="z", bufs=HN))
-        g_pool = pools.enter_context(tc.tile_pool(name="g", bufs=HN))
-        work = pools.enter_context(tc.tile_pool(name="work", bufs=3))
-        result_pool = pools.enter_context(tc.tile_pool(name="result", bufs=6))
-        psum_const = pools.enter_context(tc.psum_pool(name="psum_const", bufs=1))
-        psum = pools.enter_context(tc.psum_pool(name="psum", bufs=7))
+    with ExitStack() as stack:
+        const = stack.enter_context(tc.tile_pool(name="const", bufs=1))
+        z_pool = stack.enter_context(tc.tile_pool(name="z", bufs=HN))
+        g_pool = stack.enter_context(tc.tile_pool(name="g", bufs=HN))
+        work = stack.enter_context(tc.tile_pool(name="work", bufs=3))
+        result_pool = stack.enter_context(tc.tile_pool(name="result", bufs=6))
+        psum_const = stack.enter_context(tc.psum_pool(name="psum_const", bufs=1))
+        psum = stack.enter_context(tc.psum_pool(name="psum", bufs=7))
+        stack.enter_context(tc.manual_schedule())
 
-        z_tiles = []
-        g_tiles = []
+        z_tiles = {}
+        g_tiles = {}
         slope_tiles = {}
+        dz_row_tiles = {}
         dz_tiles = {}
 
         def load_z(n):
             z_n = z_pool.tile([P, PACK, HM], F32)
             nc.sync.dma_start(out=z_n[:], in_=z_rows[:, :, n, :])
-            z_tiles.append(z_n)
+            z_tiles[n] = z_n
 
         def load_g(n):
             g_n = g_pool.tile([P, PACK, HM], BF16)
             nc.sync.dma_start(out=g_n[:], in_=g_rows[:, :, n, :])
-            g_tiles.append(g_n)
+            g_tiles[n] = g_n
 
-        ones = const.tile([P, P], BF16)
-        nc.vector.memset(ones[:], 1.0)
         leak_rows = const.tile([P, HM], BF16)
         nc.vector.memset(leak_rows[:], 0.0)
-        nc.sync.dma_start(out=leak_rows[0:1, :], in_=leak_m.unsqueeze(0))
-        load_z(0)
-        load_z(1)
-        load_g(0)
-        x_raw = const.tile([P, PACK, IN_C], BF16)
-        nc.sync.dma_start(out=x_raw[:], in_=x_rows)
-        for n in range(1, HN):
-            if n + 1 < HN:
-                load_z(n + 1)
-            load_g(n)
-
+        nc.scalar.dma_start(out=leak_rows[0:1, :], in_=leak_m.unsqueeze(0))
+        ones = const.tile([P, P], BF16)
+        nc.vector.memset(ones[:], 1.0)
         leak_bank = psum_const.tile([P, HM], F32)
         nc.tensor.matmul(out=leak_bank[:], lhsT=ones[:], rhs=leak_rows[:], start=True, stop=True)
         leak_minus_1 = const.tile([P, HM], F32)
         nc.vector.tensor_scalar_add(out=leak_minus_1[:], in0=leak_bank[:], scalar1=-1.0)
 
+        load_z(0)
+        load_g(0)
+        load_z(1)
+        load_z(2)
+        load_g(1)
+        x_raw = const.tile([P, PACK, IN_C], BF16)
+        nc.sync.dma_start(out=x_raw[:], in_=x_rows)
+        for n in range(2, HN):
+            if n + 1 < HN:
+                load_z(n + 1)
+            load_g(n)
+
         x_grouped = const.tile([P, I_TILES, P, PACK], BF16, align_bytes=64)
-        nc.scalar.copy(out=x_grouped[:], in_=x_raw[:].rearrange("p j (q a) -> p a q j", a=I_TILES))
         x_codes = const.tile([P, IN_C], U32, align_bytes=64)
         x_scales = const.tile([P, IN_C], U8, align_bytes=64)
+
+        def regroup_x():
+            nc.scalar.copy(out=x_grouped[:], in_=x_raw[:].rearrange("p j (q a) -> p a q j", a=I_TILES))
 
         def quantise_x():
             nc.vector.quantize_mx(
@@ -107,10 +114,13 @@ def tile_tensormoe_pa_v_kernel(tc, x, W_im, W_in, leak_m, leak_n, z_m, grad_out,
                 op0=ALU.add,
                 op1=ALU.mult,
             )
+            dz_row_tiles[n] = dz_rows
+
+        def regroup(n, copy):
             dz_n = work.tile([P, HM, PACK], BF16, align_bytes=64)
-            nc.scalar.copy(
+            copy(
                 out=dz_n[:].rearrange("p (c r) j -> p c j r", r=RUN),
-                in_=dz_rows[:].rearrange("p j (c r) -> p c j r", r=RUN),
+                in_=dz_row_tiles[n][:].rearrange("p j (c r) -> p c j r", r=RUN),
             )
             dz_tiles[n] = dz_n
 
@@ -122,6 +132,8 @@ def tile_tensormoe_pa_v_kernel(tc, x, W_im, W_in, leak_m, leak_n, z_m, grad_out,
                 scales=dz_scales[:],
                 in_=dz_tiles[n][:].rearrange("p m j -> p (m j)"),
             )
+            if n == 0:
+                quantise_x()
             result = result_pool.tile([P, I_TILES, HM], F32)
             for a in range(I_TILES):
                 x_cols = slice(a * P, (a + 1) * P)
@@ -139,12 +151,17 @@ def tile_tensormoe_pa_v_kernel(tc, x, W_im, W_in, leak_m, leak_n, z_m, grad_out,
             nc.sync.dma_start(out=out[n].rearrange("(q a) m -> q a m", a=I_TILES), in_=result[:])
 
         slope_minus_1(0)
-        slope_minus_1(1)
         gradient_times_slope(0)
-        quantise_x()
+        regroup(0, nc.scalar.copy)
+        regroup_x()
+        slope_minus_1(1)
         for n in range(HN):
             if n + 2 < HN:
                 slope_minus_1(n + 2)
             if n + 1 < HN:
                 gradient_times_slope(n + 1)
+            if n + 1 < LAST:
+                regroup(n + 1, nc.scalar.copy)
+            if n == LAST:
+                regroup(n, nc.vector.tensor_copy)
             quantise_multiply_store(n)

@@ -19,6 +19,7 @@ LAST = HN - 1
 HM = 512
 I_TILES = IN_C // P
 RUN = 4
+STORE_BANKS = 2
 
 FLOPS = 2 * B * IN_C * HN * HM
 BYTES = 2 * B * IN_C + 2 * HM + 4 * B * HN * HM + 2 * B * HN * HM + 4 * HN * IN_C * HM
@@ -29,6 +30,7 @@ def tile_tensormoe_pa_v_kernel(tc, x, W_im, W_in, leak_m, leak_n, z_m, grad_out,
     x_rows = x.rearrange("(p j) i -> p j i", j=PACK)
     z_rows = z_m.rearrange("(p j) n m -> p j n m", j=PACK)
     g_rows = grad_out.rearrange("(p j) n m -> p j n m", j=PACK)
+    out_rows = out.rearrange("n (q a) m -> n q a m", a=I_TILES)
 
     with ExitStack() as stack:
         const = stack.enter_context(tc.tile_pool(name="const", bufs=1))
@@ -46,9 +48,13 @@ def tile_tensormoe_pa_v_kernel(tc, x, W_im, W_in, leak_m, leak_n, z_m, grad_out,
         dz_row_tiles = {}
         dz_tiles = {}
 
+        def z_pieces(n):
+            return ((0, 2), (2, PACK)) if n == 0 else ((0, PACK),)
+
         def load_z(n):
             z_n = z_pool.tile([P, PACK, HM], F32)
-            nc.sync.dma_start(out=z_n[:], in_=z_rows[:, :, n, :])
+            for j0, j1 in z_pieces(n):
+                nc.sync.dma_start(out=z_n[:, j0:j1, :], in_=z_rows[:, j0:j1, n, :])
             z_tiles[n] = z_n
 
         def load_g(n):
@@ -58,7 +64,7 @@ def tile_tensormoe_pa_v_kernel(tc, x, W_im, W_in, leak_m, leak_n, z_m, grad_out,
 
         leak_rows = const.tile([P, HM], BF16)
         nc.vector.memset(leak_rows[:], 0.0)
-        nc.scalar.dma_start(out=leak_rows[0:1, :], in_=leak_m.unsqueeze(0))
+        nc.sync.dma_start(out=leak_rows[0:1, :], in_=leak_m.unsqueeze(0))
         ones = const.tile([P, P], BF16)
         nc.vector.memset(ones[:], 1.0)
         leak_bank = psum_const.tile([P, HM], F32)
@@ -94,14 +100,15 @@ def tile_tensormoe_pa_v_kernel(tc, x, W_im, W_in, leak_m, leak_n, z_m, grad_out,
 
         def slope_minus_1(n):
             s_n = work.tile([P, PACK, HM], F32)
-            nc.vector.scalar_tensor_tensor(
-                out=s_n[:],
-                in0=z_tiles[n][:],
-                scalar=0.0,
-                in1=leak_minus_1[:].unsqueeze(1).to_broadcast([P, PACK, HM]),
-                op0=ALU.is_lt,
-                op1=ALU.mult,
-            )
+            for j0, j1 in z_pieces(n):
+                nc.vector.scalar_tensor_tensor(
+                    out=s_n[:, j0:j1, :],
+                    in0=z_tiles[n][:, j0:j1, :],
+                    scalar=0.0,
+                    in1=leak_minus_1[:].unsqueeze(1).to_broadcast([P, j1 - j0, HM]),
+                    op0=ALU.is_lt,
+                    op1=ALU.mult,
+                )
             slope_tiles[n] = s_n
 
         def gradient_times_slope(n):
@@ -148,7 +155,9 @@ def tile_tensormoe_pa_v_kernel(tc, x, W_im, W_in, leak_m, leak_n, z_m, grad_out,
                     stop=True,
                 )
                 nc.scalar.copy(out=result[:, a, :], in_=bank[:])
-            nc.sync.dma_start(out=out[n].rearrange("(q a) m -> q a m", a=I_TILES), in_=result[:])
+                if a % STORE_BANKS == STORE_BANKS - 1:
+                    done = slice(a + 1 - STORE_BANKS, a + 1)
+                    nc.sync.dma_start(out=out_rows[n, :, done, :], in_=result[:, done, :])
 
         slope_minus_1(0)
         gradient_times_slope(0)

@@ -24,6 +24,8 @@ STORE_BANKS = 2
 FLOPS = 2 * B * IN_C * HN * HM
 BYTES = 2 * B * IN_C + 2 * HM + 4 * B * HN * HM + 2 * B * HN * HM + 4 * HN * IN_C * HM
 
+G_COLS = 256
+
 
 def tile_tensormoe_pa_v_kernel(tc, x, W_im, W_in, leak_m, leak_n, z_m, grad_out, out):
     nc = tc.nc
@@ -47,6 +49,7 @@ def tile_tensormoe_pa_v_kernel(tc, x, W_im, W_in, leak_m, leak_n, z_m, grad_out,
         slope_tiles = {}
         dz_row_tiles = {}
         dz_tiles = {}
+        code_tiles = {}
 
         def z_pieces(n):
             return ((0, 2), (2, PACK)) if n == 0 else ((0, PACK),)
@@ -67,21 +70,22 @@ def tile_tensormoe_pa_v_kernel(tc, x, W_im, W_in, leak_m, leak_n, z_m, grad_out,
         nc.sync.dma_start(out=leak_rows[0:1, :], in_=leak_m.unsqueeze(0))
         ones = const.tile([P, P], BF16)
         nc.vector.memset(ones[:], 1.0)
-        leak_bank = psum_const.tile([P, HM], F32)
-        nc.tensor.matmul(out=leak_bank[:], lhsT=ones[:], rhs=leak_rows[:], start=True, stop=True)
-        leak_minus_1 = const.tile([P, HM], F32)
-        nc.vector.tensor_scalar_add(out=leak_minus_1[:], in0=leak_bank[:], scalar1=-1.0)
+        minus_128th = const.tile([P, HM], BF16)
+        nc.vector.memset(minus_128th[:], -1.0 / P)
+        leak_minus_1 = psum_const.tile([P, HM], F32)
+        nc.tensor.matmul(out=leak_minus_1[:], lhsT=ones[:], rhs=minus_128th[:], start=True, stop=False)
+        nc.tensor.matmul(out=leak_minus_1[:], lhsT=ones[:], rhs=leak_rows[:], start=False, stop=True)
 
         load_z(0)
         load_g(0)
         load_z(1)
-        load_z(2)
         load_g(1)
+        load_z(2)
         x_raw = const.tile([P, PACK, IN_C], BF16)
         nc.sync.dma_start(out=x_raw[:], in_=x_rows)
-        for n in range(2, HN):
-            if n + 1 < HN:
-                load_z(n + 1)
+        load_g(2)
+        for n in range(3, HN):
+            load_z(n)
             load_g(n)
 
         x_grouped = const.tile([P, I_TILES, P, PACK], BF16, align_bytes=64)
@@ -123,15 +127,29 @@ def tile_tensormoe_pa_v_kernel(tc, x, W_im, W_in, leak_m, leak_n, z_m, grad_out,
             )
             dz_row_tiles[n] = dz_rows
 
-        def regroup(n, copy):
-            dz_n = work.tile([P, HM, PACK], BF16, align_bytes=64)
+        def run_copy(copy, dz_n, n, m0, m1):
             copy(
-                out=dz_n[:].rearrange("p (c r) j -> p c j r", r=RUN),
-                in_=dz_row_tiles[n][:].rearrange("p j (c r) -> p c j r", r=RUN),
+                out=dz_n[:, m0:m1, :].rearrange("p (c r) j -> p c j r", r=RUN),
+                in_=dz_row_tiles[n][:, :, m0:m1].rearrange("p j (c r) -> p c j r", r=RUN),
             )
+
+        def regroup(n):
+            dz_n = work.tile([P, HM, PACK], BF16, align_bytes=64)
+            if n == LAST:
+                run_copy(nc.vector.tensor_copy, dz_n, n, 0, HM)
+            else:
+                nc.gpsimd.tensor_scalar(
+                    out=dz_n[:, 0:G_COLS, :],
+                    in0=dz_row_tiles[n][:, :, 0:G_COLS].rearrange("p j m -> p m j"),
+                    scalar1=1.0,
+                    scalar2=0.0,
+                    op0=ALU.mult,
+                    op1=ALU.add,
+                )
+                run_copy(nc.scalar.copy, dz_n, n, G_COLS, HM)
             dz_tiles[n] = dz_n
 
-        def quantise_multiply_store(n):
+        def quantise(n):
             dz_codes = work.tile([P, HM], U32, align_bytes=64)
             dz_scales = work.tile([P, HM], U8, align_bytes=64)
             nc.vector.quantize_mx(
@@ -139,8 +157,10 @@ def tile_tensormoe_pa_v_kernel(tc, x, W_im, W_in, leak_m, leak_n, z_m, grad_out,
                 scales=dz_scales[:],
                 in_=dz_tiles[n][:].rearrange("p m j -> p (m j)"),
             )
-            if n == 0:
-                quantise_x()
+            code_tiles[n] = (dz_codes, dz_scales)
+
+        def multiply_store(n):
+            dz_codes, dz_scales = code_tiles[n]
             result = result_pool.tile([P, I_TILES, HM], F32)
             for a in range(I_TILES):
                 x_cols = slice(a * P, (a + 1) * P)
@@ -161,16 +181,24 @@ def tile_tensormoe_pa_v_kernel(tc, x, W_im, W_in, leak_m, leak_n, z_m, grad_out,
 
         slope_minus_1(0)
         gradient_times_slope(0)
-        regroup(0, nc.scalar.copy)
+        regroup(0)
         regroup_x()
         slope_minus_1(1)
-        for n in range(HN):
-            if n + 2 < HN:
-                slope_minus_1(n + 2)
-            if n + 1 < HN:
-                gradient_times_slope(n + 1)
-            if n + 1 < LAST:
-                regroup(n + 1, nc.scalar.copy)
-            if n == LAST:
-                regroup(n, nc.vector.tensor_copy)
-            quantise_multiply_store(n)
+        gradient_times_slope(1)
+        regroup(1)
+        slope_minus_1(2)
+        for k in range(HN):
+            quantise(k)
+            if k > 0:
+                multiply_store(k)
+            if k + 2 < HN:
+                gradient_times_slope(k + 2)
+                if k + 2 < LAST:
+                    regroup(k + 2)
+            if k + 3 < HN:
+                slope_minus_1(k + 3)
+            if k == 0:
+                quantise_x()
+                multiply_store(k)
+            if k + 1 == LAST:
+                regroup(LAST)

from contextlib import ExitStack

import concourse.mybir as mybir

F32 = mybir.dt.float32
BF16 = mybir.dt.bfloat16
U32 = mybir.dt.uint32
U8 = mybir.dt.uint8
E4M3_X4 = mybir.dt.float8_e4m3fn_x4
E5M2_X4 = mybir.dt.float8_e5m2_x4
ALU = mybir.AluOpType

P = 128
PACK = 4
B = P * PACK
IN_C = 512
HN = 8
LAST = HN - 1
HM = 512
I_TILES = IN_C // P
RUN = 4
STORE_BANKS = 2

FLOPS = 2 * B * IN_C * HN * HM
BYTES = 2 * B * IN_C + 2 * HM + 4 * B * HN * HM + 2 * B * HN * HM + 4 * HN * IN_C * HM

G_COLS = 256


def tile_tensormoe_pa_v_kernel(tc, x, W_im, W_in, leak_m, leak_n, z_m, grad_out, out):
    nc = tc.nc
    x_rows = x.rearrange("(p j) i -> p j i", j=PACK)
    z_rows = z_m.rearrange("(p j) n m -> p j n m", j=PACK)
    g_rows = grad_out.rearrange("(p j) n m -> p j n m", j=PACK)
    out_rows = out.rearrange("n (q a) m -> n q a m", a=I_TILES)

    with ExitStack() as stack:
        const = stack.enter_context(tc.tile_pool(name="const", bufs=1))
        z_pool = stack.enter_context(tc.tile_pool(name="z", bufs=HN))
        g_pool = stack.enter_context(tc.tile_pool(name="g", bufs=HN))
        work = stack.enter_context(tc.tile_pool(name="work", bufs=3))
        result_pool = stack.enter_context(tc.tile_pool(name="result", bufs=6))
        psum_const = stack.enter_context(tc.psum_pool(name="psum_const", bufs=1))
        psum = stack.enter_context(tc.psum_pool(name="psum", bufs=7))
        stack.enter_context(tc.manual_schedule())

        z_tiles = {}
        g_tiles = {}
        slope_tiles = {}
        dz_row_tiles = {}
        dz_tiles = {}
        code_tiles = {}

        def z_pieces(n):
            return ((0, 2), (2, PACK)) if n == 0 else ((0, PACK),)

        def load_z(n):
            z_n = z_pool.tile([P, PACK, HM], F32)
            for j0, j1 in z_pieces(n):
                nc.sync.dma_start(out=z_n[:, j0:j1, :], in_=z_rows[:, j0:j1, n, :])
            z_tiles[n] = z_n

        def load_g(n):
            g_n = g_pool.tile([P, PACK, HM], BF16)
            nc.sync.dma_start(out=g_n[:], in_=g_rows[:, :, n, :])
            g_tiles[n] = g_n

        leak_rows = const.tile([P, HM], BF16)
        nc.vector.memset(leak_rows[:], 0.0)
        nc.sync.dma_start(out=leak_rows[0:1, :], in_=leak_m.unsqueeze(0))
        ones = const.tile([P, P], BF16)
        nc.vector.memset(ones[:], 1.0)
        minus_128th = const.tile([P, HM], BF16)
        nc.vector.memset(minus_128th[:], -1.0 / P)
        leak_minus_1 = psum_const.tile([P, HM], F32)
        nc.tensor.matmul(out=leak_minus_1[:], lhsT=ones[:], rhs=minus_128th[:], start=True, stop=False)
        nc.tensor.matmul(out=leak_minus_1[:], lhsT=ones[:], rhs=leak_rows[:], start=False, stop=True)

        load_z(0)
        load_g(0)
        load_z(1)
        load_g(1)
        load_z(2)
        x_raw = const.tile([P, PACK, IN_C], BF16)
        nc.sync.dma_start(out=x_raw[:], in_=x_rows)
        load_g(2)
        for n in range(3, HN):
            load_z(n)
            load_g(n)

        x_grouped = const.tile([P, I_TILES, P, PACK], BF16, align_bytes=64)
        x_codes = const.tile([P, IN_C], U32, align_bytes=64)
        x_scales = const.tile([P, IN_C], U8, align_bytes=64)

        def regroup_x():
            nc.scalar.copy(out=x_grouped[:], in_=x_raw[:].rearrange("p j (q a) -> p a q j", a=I_TILES))

        def quantise_x():
            nc.vector.quantize_mx(
                out=x_codes[:].bitcast(E4M3_X4),
                scales=x_scales[:],
                in_=x_grouped[:].rearrange("p a q j -> p (a q j)"),
            )

        def slope_minus_1(n):
            s_n = work.tile([P, PACK, HM], F32)
            for j0, j1 in z_pieces(n):
                nc.vector.scalar_tensor_tensor(
                    out=s_n[:, j0:j1, :],
                    in0=z_tiles[n][:, j0:j1, :],
                    scalar=0.0,
                    in1=leak_minus_1[:].unsqueeze(1).to_broadcast([P, j1 - j0, HM]),
                    op0=ALU.is_lt,
                    op1=ALU.mult,
                )
            slope_tiles[n] = s_n

        def gradient_times_slope(n):
            dz_rows = work.tile([P, PACK, HM], BF16)
            nc.vector.scalar_tensor_tensor(
                out=dz_rows[:],
                in0=slope_tiles[n][:],
                scalar=1.0,
                in1=g_tiles[n][:],
                op0=ALU.add,
                op1=ALU.mult,
            )
            dz_row_tiles[n] = dz_rows

        def run_copy(copy, dz_n, n, m0, m1):
            copy(
                out=dz_n[:, m0:m1, :].rearrange("p (c r) j -> p c j r", r=RUN),
                in_=dz_row_tiles[n][:, :, m0:m1].rearrange("p j (c r) -> p c j r", r=RUN),
            )

        def regroup(n):
            dz_n = work.tile([P, HM, PACK], BF16, align_bytes=64)
            if n == LAST:
                run_copy(nc.vector.tensor_copy, dz_n, n, 0, HM)
            else:
                nc.gpsimd.tensor_scalar(
                    out=dz_n[:, 0:G_COLS, :],
                    in0=dz_row_tiles[n][:, :, 0:G_COLS].rearrange("p j m -> p m j"),
                    scalar1=1.0,
                    scalar2=0.0,
                    op0=ALU.mult,
                    op1=ALU.add,
                )
                run_copy(nc.scalar.copy, dz_n, n, G_COLS, HM)
            dz_tiles[n] = dz_n

        def quantise(n):
            dz_codes = work.tile([P, HM], U32, align_bytes=64)
            dz_scales = work.tile([P, HM], U8, align_bytes=64)
            nc.vector.quantize_mx(
                out=dz_codes[:].bitcast(E5M2_X4),
                scales=dz_scales[:],
                in_=dz_tiles[n][:].rearrange("p m j -> p (m j)"),
            )
            code_tiles[n] = (dz_codes, dz_scales)

        def multiply_store(n):
            dz_codes, dz_scales = code_tiles[n]
            result = result_pool.tile([P, I_TILES, HM], F32)
            for a in range(I_TILES):
                x_cols = slice(a * P, (a + 1) * P)
                bank = psum.tile([P, HM], F32)
                nc.tensor.matmul_mx(
                    out=bank[:],
                    lhsT=x_codes[:, x_cols].bitcast(E4M3_X4),
                    lhsT_scale=x_scales[:, x_cols],
                    rhs=dz_codes[:].bitcast(E5M2_X4),
                    rhs_scale=dz_scales[:],
                    start=True,
                    stop=True,
                )
                nc.scalar.copy(out=result[:, a, :], in_=bank[:])
                if a % STORE_BANKS == STORE_BANKS - 1:
                    done = slice(a + 1 - STORE_BANKS, a + 1)
                    nc.sync.dma_start(out=out_rows[n, :, done, :], in_=result[:, done, :])

        slope_minus_1(0)
        gradient_times_slope(0)
        regroup(0)
        regroup_x()
        slope_minus_1(1)
        gradient_times_slope(1)
        regroup(1)
        slope_minus_1(2)
        for k in range(HN):
            quantise(k)
            if k > 0:
                multiply_store(k)
            if k + 2 < HN:
                gradient_times_slope(k + 2)
                if k + 2 < LAST:
                    regroup(k + 2)
            if k + 3 < HN:
                slope_minus_1(k + 3)
            if k == 0:
                quantise_x()
                multiply_store(k)
            if k + 1 == LAST:
                regroup(LAST)
